import numpy as np
import ml_dtypes


def mxq(x, axis, fmt="e4m3"):
    dtype, down = {"e4m3": (ml_dtypes.float8_e4m3fn, 7), "e5m2": (ml_dtypes.float8_e5m2, 14)}[fmt]
    v = np.moveaxis(np.asarray(x, np.float32).astype(ml_dtypes.bfloat16).astype(np.float64), axis, -1)
    blocks = v.reshape(v.shape[:-1] + (-1, 32))
    amax = np.abs(blocks).max(-1, keepdims=True)
    byte = np.maximum(np.where(amax > 0, np.frexp(amax)[1] - 1 + 127, 0) - down, 1)
    scale = np.exp2(byte - 127.0)
    codes = (blocks / scale).astype(np.float32).astype(dtype).astype(np.float64)
    return np.moveaxis((codes * scale).reshape(v.shape), -1, axis)


WIDE = False


def mx_kscale(k):
    if not WIDE:
        return np.ones(k)
    levels = np.array([10, -10, 5, -5, 0])
    a = np.random.permutation(np.resize(levels, k // 512 * 4)).reshape(k // 512, 4)
    idx = np.arange(k)
    return np.exp2(a[idx // 512, idx % 128 // 32])


BF16 = ml_dtypes.bfloat16


def bf(x):
    return np.asarray(x, np.float32).astype(BF16)


def f64(x):
    return np.asarray(x).astype(np.float64)


E2M1 = np.array([0.0, 0.5, 1.0, 1.5, 2.0, 3.0, 4.0, 6.0, -0.0, -0.5, -1.0, -1.5, -2.0, -3.0, -4.0, -6.0])


def pack_weight(w, fmt):
    k, n = w.shape
    w = f64(bf(w)).reshape(k // 32, 32, n)
    amax = np.abs(w).max(1)
    if fmt == "e4m3":
        byte = np.frexp(amax)[1] - 1 + 127 - 7
    else:
        mant, ex = np.frexp(amax / 6.0)
        byte = np.where(mant > 0.5, ex, ex - 1) + 127
    byte = np.clip(np.where(amax > 0, byte, 1), 1, 254)
    scaled = (w * np.exp2(127.0 - byte)[:, None, :]).reshape(k, n).astype(np.float32)
    by_word = np.ascontiguousarray(scaled.reshape(k // 512, 128, 4, n).transpose(0, 1, 3, 2))
    if fmt == "e4m3":
        words = by_word.astype(ml_dtypes.float8_e4m3fn).view(np.uint8)
    else:
        c = by_word.astype(ml_dtypes.float4_e2m1fn).view(np.uint8) & 0xF
        words = c[..., 0::2] | (c[..., 1::2] << 4)
    return np.ascontiguousarray(words), np.ascontiguousarray(byte.astype(np.uint8).reshape(k // 512, 16, n))


def unpack_weight(words, scales, fmt):
    g, p, n, _ = words.shape
    if fmt == "e4m3":
        vals = np.ascontiguousarray(words).view(ml_dtypes.float8_e4m3fn).astype(np.float64)
    else:
        nib = np.empty((g, p, n, 4), np.uint8)
        nib[..., 0::2] = words & 0xF
        nib[..., 1::2] = words >> 4
        vals = E2M1[nib]
    vals = vals * np.repeat(np.exp2(scales.astype(np.float64) - 127.0), 8, axis=1)[..., None]
    return vals.transpose(0, 1, 3, 2).reshape(g * 512, n)


B, I, N, M = 128, 1024, 1024, 4
K = I + N
NM = N * M
FMT = "e4m3"


def sigmoid(v):
    return 1.0 / (1.0 + np.exp(-v))


def softmax(v):
    e = np.exp(v - v.max())
    return e / e.sum()


def setup_inputs():
    s = mx_kscale(K)[:I]
    d = np.concatenate([s, np.ones(N)])[:, None]
    inputs = bf(np.random.standard_normal((B, I)) * s)
    state = bf(np.random.standard_normal((B, NM)) / np.sqrt(M))
    W_z_words, W_z_scales = pack_weight(np.random.standard_normal((K, NM)) / np.sqrt(K) / d, FMT)
    b_z = bf(np.random.standard_normal(NM) * 0.1)
    W_r_words, W_r_scales = pack_weight(np.random.standard_normal((K, NM)) / np.sqrt(K) / d, FMT)
    b_r = bf(np.random.standard_normal(NM) * 0.1)
    W_h_words, W_h_scales = pack_weight(np.random.standard_normal((K, NM)) / np.sqrt(K) / d, FMT)
    b_h = bf(np.random.standard_normal(NM) * 0.1)
    return {'inputs': inputs,
            'state': state,
            'W_z_words': W_z_words,
            'W_z_scales': W_z_scales,
            'b_z': b_z,
            'W_r_words': W_r_words,
            'W_r_scales': W_r_scales,
            'b_r': b_r,
            'W_h_words': W_h_words,
            'W_h_scales': W_h_scales,
            'b_h': b_h}


def reference(inputs, state, W_z_words, W_z_scales, b_z, W_r_words, W_r_scales, b_r, W_h_words, W_h_scales, b_h):
    x = f64(inputs)
    Wz = unpack_weight(W_z_words, W_z_scales, FMT)
    Wr = unpack_weight(W_r_words, W_r_scales, FMT)
    Wh = unpack_weight(W_h_words, W_h_scales, FMT)
    Bb, input_size = x.shape
    n = Wz.shape[0] - input_size
    m = Wz.shape[1] // n
    ln_tau = 0.5 * np.log(10.0) * np.arange(m, dtype=np.float64)
    alpha = softmax(-ln_tau)
    h = f64(state).reshape(Bb, n, m)
    h_sum = h.sum(axis=2)
    fq = mxq(np.concatenate([x, h_sum], axis=-1), 1, 'e4m3')
    z = sigmoid((fq @ Wz) + f64(b_z)).reshape(Bb, n, m)
    r = sigmoid((fq @ Wr) + f64(b_r)).reshape(Bb, n, m)
    r_h = (r * h).sum(axis=2)
    frq = mxq(np.concatenate([x, r_h], axis=-1), 1, 'e4m3')
    h_hat = np.tanh((frq @ Wh) + f64(b_h)).reshape(Bb, n, m)
    h_new = (1.0 - z) * h + z * alpha * h_hat
    output = h_new.sum(axis=2)
    new_state = h_new.reshape(Bb, n * m)
    return output, new_state

@@ -1,0 +1,274 @@
+from contextlib import ExitStack
+
+import concourse.mybir as mybir
+from concourse.masks import make_identity
+
+F32 = mybir.dt.float32
+BF16 = mybir.dt.bfloat16
+I32 = mybir.dt.int32
+U32 = mybir.dt.uint32
+U8 = mybir.dt.uint8
+FP8X4 = mybir.dt.float8_e4m3fn_x4
+ALU = mybir.AluOpType
+ACT = mybir.ActivationFunctionType
+AX = mybir.AxisListType
+
+P = 128
+I_IN = 1024
+UNITS = 1024
+M = 4
+NM = UNITS * M
+BANK = 512
+RING = 10
+
+FLOPS = 2 * 128 * 2048 * 4096 * 3
+
+
+def tile_ctgrucell_w_kernel(
+    tc, inputs, state, W_z_words, W_z_scales, b_z, W_r_words, W_r_scales, b_r,
+    W_h_words, W_h_scales, b_h, out_0, out_1,
+):
+    nc = tc.nc
+    raw = [10.0 ** (-0.5 * m) for m in range(M)]
+    alpha = [v / sum(raw) for v in raw]
+    words = {"r": W_r_words, "z": W_z_words, "h": W_h_words}
+    scales = {"r": W_r_scales, "z": W_z_scales, "h": W_h_scales}
+    biases = {"r": b_r, "z": b_z, "h": b_h}
+    order = ("r", "z", "h")
+
+    chunks = []
+
+    def pair(w, gp, j):
+        chunks.append((w, "pair", gp, j,
+                       [(2 * gp + gi, 2 * j + b, 1024 * gi + BANK * b) for gi in range(2) for b in range(2)]))
+
+    for gp, j in ((0, 0), (0, 1), (1, 0), (1, 1), (0, 2), (1, 2), (0, 3), (1, 3)):
+        pair("r", gp, j)
+    for j in range(4):
+        for gp in range(2):
+            pair("z", gp, j)
+    for j in range(3):
+        for gp in range(2):
+            pair("h", gp, j)
+    for bank in (6, 7):
+        chunks.append(("h", "bank", 0, bank, [(g, bank, BANK * g) for g in range(4)]))
+
+    with ExitStack() as ctx:
+        ctx.enter_context(nc.allow_low_precision(reason="sums are made in float32 and rounded once to bfloat16"))
+        keep = ctx.enter_context(tc.tile_pool(name="keep", bufs=1))
+        ring = ctx.enter_context(tc.tile_pool(name="ring", bufs=RING))
+        work = ctx.enter_context(tc.tile_pool(name="work", bufs=3))
+        psum = ctx.enter_context(tc.psum_pool(name="psum", bufs=6))
+        aux = ctx.enter_context(tc.psum_pool(name="aux", bufs=2))
+
+        planes = {}
+        for w in order:
+            planes[w] = keep.tile([P, NM], U8, name="planes_" + w, align_bytes=64)
+            nc.vector.memset(planes[w][:].bitcast(I32), 0)
+        brow = keep.tile([P, NM], BF16, name="brow")
+        nc.vector.memset(brow[:].bitcast(I32), 0)
+
+        def load_scales(w):
+            for q in range(4):
+                nc.sync.dma_start(
+                    out=planes[w][32 * q:32 * q + 16, :].bitcast(I32),
+                    in_=scales[w][:, 4 * q:4 * q + 4, :].bitcast(I32),
+                )
+
+        x_sb = keep.tile([P, I_IN], BF16, name="x_sb")
+        nc.scalar.dma_start(out=x_sb[:], in_=inputs)
+        h_sb = keep.tile([P, NM], BF16, name="h_sb")
+        for half in range(2):
+            nc.scalar.dma_start(out=h_sb[:, 2048 * half:2048 * (half + 1)], in_=state[:, 2048 * half:2048 * (half + 1)])
+        for j, w in enumerate(order):
+            nc.scalar.dma_start(out=brow[j:j + 1, :], in_=biases[w].unsqueeze(0))
+
+        tiles = {}
+
+        def load(i):
+            w, kind, a, b, plist = chunks[i]
+            if i == 0:
+                load_scales("r")
+            elif i == 4:
+                load_scales("z")
+            elif i == 12:
+                load_scales("h")
+            t = ring.tile([P, 2048], U32, name="w%d" % i, tag="w", align_bytes=64)
+            tiles[i] = t
+            if kind == "pair":
+                src = words[w].rearrange("g p n t -> p g (n t)")[:, 2 * a:2 * a + 2, 4096 * b:4096 * (b + 1)].bitcast(I32)
+                dst = t[:].bitcast(I32).rearrange("p (g c) -> p g c", g=2)
+            else:
+                src = words[w].rearrange("g p n t -> p g (n t)")[:, :, 2048 * b:2048 * (b + 1)].bitcast(I32)
+                dst = t[:].bitcast(I32).rearrange("p (g c) -> p g c", g=4)
+            nc.sync.dma_start(out=dst, in_=src)
+
+        for i in range(RING):
+            load(i)
+
+        ident_f = keep.tile([P, P], F32, name="ident_f")
+        make_identity(nc, ident_f[:])
+        ident_b = keep.tile([P, P], BF16, name="ident_b")
+        make_identity(nc, ident_b[:])
+        ones = keep.tile([P, P], F32, name="ones")
+        nc.gpsimd.memset(ones[:], 1.0)
+        alpha_t = keep.tile([P, P, M], F32, name="alpha_t")
+        for m in range(M):
+            nc.gpsimd.tensor_scalar(out=alpha_t[:, :, m], in0=ones[:], scalar1=alpha[m], scalar2=0.0,
+                                    op0=ALU.mult, op1=ALU.add)
+        alpha_flat = alpha_t[:].rearrange("p n m -> p (n m)")
+        warm = keep.tile([P, 1], F32, name="warm")
+        nc.scalar.activation(out=warm[:], in_=ones[:, 0:1], func=ACT.Sigmoid)
+
+        codes = keep.tile([P, 4 * P], U32, name="codes", align_bytes=64)
+        ascl = keep.tile([P, 4 * P], U8, name="ascl", align_bytes=64)
+        codes_r = keep.tile([P, 2 * P], U32, name="codes_r", align_bytes=64)
+        ascl_r = keep.tile([P, 2 * P], U8, name="ascl_r", align_bytes=64)
+        bias_bc = {}
+        for w in order:
+            bias_bc[w] = keep.tile([P, NM], BF16, name="bias_" + w)
+        neg_a = keep.tile([P, NM], F32, name="neg_a")
+        za = keep.tile([P, NM], F32, name="za")
+        hs = keep.tile([P, UNITS], BF16, name="hs")
+        rhb = keep.tile([P, UNITS], BF16, name="rhb")
+        o0 = keep.tile([P, UNITS], F32, name="o0")
+
+        def spread_bias(w):
+            j = order.index(w)
+            for q in range(4):
+                bp = aux.tile([P, 1024], BF16, name="bp", tag="aux")
+                for hh in range(2):
+                    nc.tensor.matmul(
+                        out=bp[:, BANK * hh:BANK * (hh + 1)],
+                        lhsT=ident_b[:, j:j + 1].to_broadcast([P, P]),
+                        rhs=brow[:, 1024 * q + BANK * hh:1024 * q + BANK * (hh + 1)],
+                        start=True, stop=True,
+                    )
+                nc.scalar.copy(out=bias_bc[w][:, 1024 * q:1024 * (q + 1)], in_=bp[:])
+
+        def flip_units(src, half):
+            tp = aux.tile([P, 4, P], BF16, name="tp", tag="aux")
+            for t in range(4):
+                nc.tensor.transpose(tp[:, t, :], src[:, 512 * half + t:512 * (half + 1):4], ident_b[:])
+            return tp
+
+        def group_units(engine_copy, tp):
+            grp = work.tile([P, BANK], BF16, name="grp", tag="grp", bufs=2, align_bytes=64)
+            engine_copy(out=grp[:].rearrange("p (b t) -> p b t", t=4), in_=tp[:].rearrange("p t b -> p b t"))
+            return grp
+
+        def quantise(grp, c_out, s_out):
+            nc.vector.quantize_mx(out=c_out.bitcast(FP8X4), scales=s_out, in_=grp[:])
+
+        def sum_state(half):
+            nc.vector.tensor_reduce(out=hs[:, 512 * half:512 * (half + 1)],
+                                    in_=h_sb[:, 2048 * half:2048 * (half + 1)].rearrange("p (n m) -> p n m", m=M),
+                                    axis=AX.X, op=ALU.add)
+
+        xw = x_sb[:].bitcast(F32)
+        tpx = aux.tile([P, 2, 2, P], F32, name="tpx", tag="aux")
+        for g in range(2):
+            for u in range(2):
+                nc.tensor.transpose(tpx[:, g, u, :], xw[:, 256 * g + u:256 * (g + 1):2], ident_f[:])
+        gx = keep.tile([P, 1024], BF16, name="gx", align_bytes=64)
+        nc.vector.tensor_copy(
+            out=gx[:].bitcast(F32).rearrange("p (g b u) -> p g b u", g=2, u=2),
+            in_=tpx[:].rearrange("p g u b -> p g b u"),
+        )
+        sum_state(0)
+        nc.vector.quantize_mx(out=codes[:, 0:256].bitcast(FP8X4), scales=ascl[:, 0:256], in_=gx[:])
+        tp0 = flip_units(hs, 0)
+        sum_state(1)
+        grp0 = group_units(nc.vector.tensor_copy, tp0)
+        tp1 = flip_units(hs, 1)
+        grp1 = group_units(nc.vector.tensor_copy, tp1)
+        quantise(grp0, codes[:, 256:384], ascl[:, 256:384])
+        quantise(grp1, codes[:, 384:512], ascl[:, 384:512])
+        spread_bias("r")
+
+        acc = {}
+
+        def passes(i):
+            w, kind, a, b, plist = chunks[i]
+            t = tiles[i]
+            for g, bank, off in plist:
+                if g == 0:
+                    acc[bank] = psum.tile([P, BANK], F32, name="acc_%s%d" % (w, bank), tag="acc")
+                if w == "h" and g >= 2:
+                    lw = codes_r[:, P * (g - 2):P * (g - 1)]
+                    ls = ascl_r[:, P * (g - 2):P * (g - 1)]
+                else:
+                    lw = codes[:, P * g:P * (g + 1)]
+                    ls = ascl[:, P * g:P * (g + 1)]
+                nc.tensor.matmul_mx(
+                    out=acc[bank][:],
+                    lhsT=lw.bitcast(FP8X4), lhsT_scale=ls,
+                    rhs=t[:, off:off + BANK].bitcast(FP8X4),
+                    rhs_scale=planes[w][4 * g:P, BANK * bank:BANK * (bank + 1)],
+                    start=(g == 0), stop=(g == 3),
+                )
+
+        def front(w, bank, func):
+            cols = slice(BANK * bank, BANK * (bank + 1))
+            vb = work.tile([P, BANK], F32, name="vb", tag="vb", bufs=4)
+            nc.vector.tensor_tensor(out=vb[:], in0=acc[bank][:], in1=bias_bc[w][:, cols], op=ALU.add)
+            a = work.tile([P, BANK], F32, name="a", tag="act", bufs=4)
+            nc.scalar.activation(out=a[:], in_=vb[:], func=func)
+            return a
+
+        def back_r(bank, r):
+            cols = slice(BANK * bank, BANK * (bank + 1))
+            rh = work.tile([P, BANK], F32, name="rh", tag="prod", bufs=3)
+            nc.vector.tensor_tensor(out=rh[:], in0=r[:], in1=h_sb[:, cols], op=ALU.mult)
+            nc.vector.tensor_reduce(out=rhb[:, P * bank:P * (bank + 1)],
+                                    in_=rh[:].rearrange("p (n m) -> p n m", m=M), axis=AX.X, op=ALU.add)
+
+        def back_z(bank, z):
+            cols = slice(BANK * bank, BANK * (bank + 1))
+            nc.vector.scalar_tensor_tensor(out=neg_a[:, cols], in0=z[:], scalar=1.0, in1=h_sb[:, cols],
+                                           op0=ALU.subtract, op1=ALU.mult)
+            nc.gpsimd.tensor_tensor(out=za[:, cols], in0=z[:], in1=alpha_flat, op=ALU.mult)
+
+        def back_h(bank, hh):
+            cols = slice(BANK * bank, BANK * (bank + 1))
+            t1 = work.tile([P, BANK], F32, name="t1", tag="prod", bufs=3)
+            nc.vector.tensor_tensor(out=t1[:], in0=hh[:], in1=za[:, cols], op=ALU.mult)
+            hn = work.tile([P, BANK], F32, name="hn", tag="hn", bufs=4)
+            nc.vector.tensor_tensor(out=hn[:], in0=t1[:], in1=neg_a[:, cols], op=ALU.subtract)
+            queue = nc.gpsimd if bank < 6 else nc.sync
+            queue.dma_start(out=out_1[:, cols], in_=hn[:])
+            nc.vector.tensor_reduce(out=o0[:, P * bank:P * (bank + 1)],
+                                    in_=hn[:].rearrange("p (n m) -> p n m", m=M), axis=AX.X, op=ALU.add)
+            if bank == 3:
+                nc.gpsimd.dma_start(out=out_0[:, 0:512], in_=o0[:, 0:512])
+            elif bank == 5:
+                nc.gpsimd.dma_start(out=out_0[:, 512:768], in_=o0[:, 512:768])
+            elif bank >= 6:
+                nc.sync.dma_start(out=out_0[:, P * bank:P * (bank + 1)], in_=o0[:, P * bank:P * (bank + 1)])
+
+        backs = {"r": back_r, "z": back_z, "h": back_h}
+        funcs = {"r": ACT.Sigmoid, "z": ACT.Sigmoid, "h": ACT.Tanh}
+        flips = {5: 0, 9: 1}
+
+        for i in range(len(chunks)):
+            passes(i)
+            if i + RING < len(chunks):
+                load(i + RING)
+            tp = None
+            if i in flips:
+                tp = flip_units(rhb, flips[i])
+            w = chunks[i][0]
+            closed = [bank for g, bank, off in chunks[i][4] if g == 3]
+            outs = [front(w, bank, funcs[w]) for bank in closed]
+            grp = None
+            if i in flips:
+                grp = group_units(nc.scalar.copy, tp)
+            if i == 1:
+                spread_bias("z")
+            if i == 4:
+                spread_bias("h")
+            for bank, a in zip(closed, outs):
+                backs[w](bank, a)
+            if i in flips:
+                half = flips[i]
+                quantise(grp, codes_r[:, P * half:P * (half + 1)], ascl_r[:, P * half:P * (half + 1)])

@@ -19,7 +19,8 @@ UNITS = 1024
 M = 4
 NM = UNITS * M
 BANK = 512
-RING = 10
+RING = 6
+LAG = 2
 
 FLOPS = 2 * 128 * 2048 * 4096 * 3
 
@@ -36,37 +37,32 @@ def tile_ctgrucell_w_kernel(
     biases = {"r": b_r, "z": b_z, "h": b_h}
     order = ("r", "z", "h")
 
-    chunks = []
-
-    def pair(w, gp, j):
-        chunks.append((w, "pair", gp, j,
-                       [(2 * gp + gi, 2 * j + b, 1024 * gi + BANK * b) for gi in range(2) for b in range(2)]))
-
-    for gp, j in ((0, 0), (0, 1), (1, 0), (1, 1), (0, 2), (1, 2), (0, 3), (1, 3)):
-        pair("r", gp, j)
-    for j in range(4):
-        for gp in range(2):
-            pair("z", gp, j)
+    blocks = []
+    for w in ("r", "z"):
+        for j in range(4):
+            blocks.append((w, 1024 * j, 1024))
     for j in range(3):
-        for gp in range(2):
-            pair("h", gp, j)
-    for bank in (6, 7):
-        chunks.append(("h", "bank", 0, bank, [(g, bank, BANK * g) for g in range(4)]))
+        blocks.append(("h", 1024 * j, 1024))
+    blocks.append(("h", 3072, 512))
+    blocks.append(("h", 3584, 512))
+    banks = []
+    for k, (w, c0, ncols) in enumerate(blocks):
+        for i in range(ncols // BANK):
+            banks.append((w, c0 // BANK + i, k, BANK * i, i == ncols // BANK - 1))
 
     with ExitStack() as ctx:
         ctx.enter_context(nc.allow_low_precision(reason="sums are made in float32 and rounded once to bfloat16"))
         keep = ctx.enter_context(tc.tile_pool(name="keep", bufs=1))
         ring = ctx.enter_context(tc.tile_pool(name="ring", bufs=RING))
         work = ctx.enter_context(tc.tile_pool(name="work", bufs=3))
-        psum = ctx.enter_context(tc.psum_pool(name="psum", bufs=6))
-        aux = ctx.enter_context(tc.psum_pool(name="aux", bufs=2))
+        psum = ctx.enter_context(tc.psum_pool(name="psum", bufs=3))
 
         planes = {}
         for w in order:
             planes[w] = keep.tile([P, NM], U8, name="planes_" + w, align_bytes=64)
             nc.vector.memset(planes[w][:].bitcast(I32), 0)
-        brow = keep.tile([P, NM], BF16, name="brow")
-        nc.vector.memset(brow[:].bitcast(I32), 0)
+        bsrc = keep.tile([P, P], BF16, name="bsrc")
+        nc.vector.memset(bsrc[:], 0.0)
 
         def load_scales(w):
             for q in range(4):
@@ -81,42 +77,38 @@ def tile_ctgrucell_w_kernel(
         for half in range(2):
             nc.scalar.dma_start(out=h_sb[:, 2048 * half:2048 * (half + 1)], in_=state[:, 2048 * half:2048 * (half + 1)])
         for j, w in enumerate(order):
-            nc.scalar.dma_start(out=brow[j:j + 1, :], in_=biases[w].unsqueeze(0))
+            nc.scalar.dma_start(out=bsrc[32 * j:32 * (j + 1), :], in_=biases[w].rearrange("(c p) -> c p", p=P))
 
         tiles = {}
 
-        def load(i):
-            w, kind, a, b, plist = chunks[i]
-            if i == 0:
+        def load(k):
+            w, c0, ncols = blocks[k]
+            if k == 0:
                 load_scales("r")
-            elif i == 4:
+            elif k == 2:
                 load_scales("z")
-            elif i == 12:
+            elif k == 6:
                 load_scales("h")
-            t = ring.tile([P, 2048], U32, name="w%d" % i, tag="w", align_bytes=64)
-            tiles[i] = t
-            if kind == "pair":
-                src = words[w].rearrange("g p n t -> p g (n t)")[:, 2 * a:2 * a + 2, 4096 * b:4096 * (b + 1)].bitcast(I32)
-                dst = t[:].bitcast(I32).rearrange("p (g c) -> p g c", g=2)
-            else:
-                src = words[w].rearrange("g p n t -> p g (n t)")[:, :, 2048 * b:2048 * (b + 1)].bitcast(I32)
-                dst = t[:].bitcast(I32).rearrange("p (g c) -> p g c", g=4)
-            nc.sync.dma_start(out=dst, in_=src)
+            t = ring.tile([P, 4, ncols], U32, name="w%d" % k, tag="w", align_bytes=64)
+            tiles[k] = t
+            nc.sync.dma_start(
+                out=t[:].bitcast(I32),
+                in_=words[w].rearrange("g p n t -> p g (n t)")[:, :, 4 * c0:4 * (c0 + ncols)].bitcast(I32),
+            )
 
-        for i in range(RING):
-            load(i)
+        for k in range(RING):
+            load(k)
 
         ident_f = keep.tile([P, P], F32, name="ident_f")
         make_identity(nc, ident_f[:])
         ident_b = keep.tile([P, P], BF16, name="ident_b")
         make_identity(nc, ident_b[:])
-        ones = keep.tile([P, P], F32, name="ones")
+        ones = keep.tile([P, 32], F32, name="ones")
         nc.gpsimd.memset(ones[:], 1.0)
-        alpha_t = keep.tile([P, P, M], F32, name="alpha_t")
+        alpha_row = keep.tile([P, 32, M], F32, name="alpha_row")
         for m in range(M):
-            nc.gpsimd.tensor_scalar(out=alpha_t[:, :, m], in0=ones[:], scalar1=alpha[m], scalar2=0.0,
+            nc.gpsimd.tensor_scalar(out=alpha_row[:, :, m], in0=ones[:], scalar1=alpha[m], scalar2=0.0,
                                     op0=ALU.mult, op1=ALU.add)
-        alpha_flat = alpha_t[:].rearrange("p n m -> p (n m)")
         warm = keep.tile([P, 1], F32, name="warm")
         nc.scalar.activation(out=warm[:], in_=ones[:, 0:1], func=ACT.Sigmoid)
 
@@ -124,30 +116,17 @@ def tile_ctgrucell_w_kernel(
         ascl = keep.tile([P, 4 * P], U8, name="ascl", align_bytes=64)
         codes_r = keep.tile([P, 2 * P], U32, name="codes_r", align_bytes=64)
         ascl_r = keep.tile([P, 2 * P], U8, name="ascl_r", align_bytes=64)
-        bias_bc = {}
-        for w in order:
-            bias_bc[w] = keep.tile([P, NM], BF16, name="bias_" + w)
-        neg_a = keep.tile([P, NM], F32, name="neg_a")
-        za = keep.tile([P, NM], F32, name="za")
+        bias_pp = keep.tile([P, P], F32, name="bias_pp")
+        alpha_pp = keep.tile([P, 1], F32, name="alpha_pp")
+        h_t = keep.tile([P, 32, P], BF16, name="h_t")
+        z_t = keep.tile([P, 32, P], F32, name="z_t")
+        neg_a = keep.tile([P, 32, P], F32, name="neg_a")
         hs = keep.tile([P, UNITS], BF16, name="hs")
         rhb = keep.tile([P, UNITS], BF16, name="rhb")
         o0 = keep.tile([P, UNITS], F32, name="o0")
 
-        def spread_bias(w):
-            j = order.index(w)
-            for q in range(4):
-                bp = aux.tile([P, 1024], BF16, name="bp", tag="aux")
-                for hh in range(2):
-                    nc.tensor.matmul(
-                        out=bp[:, BANK * hh:BANK * (hh + 1)],
-                        lhsT=ident_b[:, j:j + 1].to_broadcast([P, P]),
-                        rhs=brow[:, 1024 * q + BANK * hh:1024 * q + BANK * (hh + 1)],
-                        start=True, stop=True,
-                    )
-                nc.scalar.copy(out=bias_bc[w][:, 1024 * q:1024 * (q + 1)], in_=bp[:])
-
         def flip_units(src, half):
-            tp = aux.tile([P, 4, P], BF16, name="tp", tag="aux")
+            tp = psum.tile([P, 4, P], BF16, name="tp", tag="aux", bufs=2)
             for t in range(4):
                 nc.tensor.transpose(tp[:, t, :], src[:, 512 * half + t:512 * (half + 1):4], ident_b[:])
             return tp
@@ -166,7 +145,7 @@ def tile_ctgrucell_w_kernel(
                                     axis=AX.X, op=ALU.add)
 
         xw = x_sb[:].bitcast(F32)
-        tpx = aux.tile([P, 2, 2, P], F32, name="tpx", tag="aux")
+        tpx = psum.tile([P, 2, 2, P], F32, name="tpx", tag="aux", bufs=2)
         for g in range(2):
             for u in range(2):
                 nc.tensor.transpose(tpx[:, g, u, :], xw[:, 256 * g + u:256 * (g + 1):2], ident_f[:])
@@ -184,91 +163,119 @@ def tile_ctgrucell_w_kernel(
         grp1 = group_units(nc.vector.tensor_copy, tp1)
         quantise(grp0, codes[:, 256:384], ascl[:, 256:384])
         quantise(grp1, codes[:, 384:512], ascl[:, 384:512])
-        spread_bias("r")
+        tpb = psum.tile([P, P], BF16, name="tpb", tag="tb")
+        nc.tensor.transpose(tpb[:], bsrc[:], ident_b[:])
+        nc.scalar.copy(out=bias_pp[:], in_=tpb[:])
+        tpa = psum.tile([P, P], F32, name="tpa", tag="tb")
+        nc.tensor.transpose(tpa[:], alpha_row[:].rearrange("p n m -> p (n m)"), ident_f[:])
+        nc.scalar.copy(out=alpha_pp[:], in_=tpa[:, 0:1])
+        for q in range(4):
+            tph = psum.tile([P, 8, P], BF16, name="tph", tag="tb")
+            for c in range(8):
+                nc.tensor.transpose(tph[:, c, :], h_sb[:, P * (8 * q + c):P * (8 * q + c + 1)], ident_b[:])
+            nc.scalar.copy(out=h_t[:, 8 * q:8 * (q + 1), :], in_=tph[:])
 
-        acc = {}
-
-        def passes(i):
-            w, kind, a, b, plist = chunks[i]
-            t = tiles[i]
-            for g, bank, off in plist:
-                if g == 0:
-                    acc[bank] = psum.tile([P, BANK], F32, name="acc_%s%d" % (w, bank), tag="acc")
-                if w == "h" and g >= 2:
-                    lw = codes_r[:, P * (g - 2):P * (g - 1)]
-                    ls = ascl_r[:, P * (g - 2):P * (g - 1)]
-                else:
-                    lw = codes[:, P * g:P * (g + 1)]
-                    ls = ascl[:, P * g:P * (g + 1)]
-                nc.tensor.matmul_mx(
-                    out=acc[bank][:],
-                    lhsT=lw.bitcast(FP8X4), lhsT_scale=ls,
-                    rhs=t[:, off:off + BANK].bitcast(FP8X4),
-                    rhs_scale=planes[w][4 * g:P, BANK * bank:BANK * (bank + 1)],
-                    start=(g == 0), stop=(g == 3),
-                )
-
-        def front(w, bank, func):
-            cols = slice(BANK * bank, BANK * (bank + 1))
-            vb = work.tile([P, BANK], F32, name="vb", tag="vb", bufs=4)
-            nc.vector.tensor_tensor(out=vb[:], in0=acc[bank][:], in1=bias_bc[w][:, cols], op=ALU.add)
-            a = work.tile([P, BANK], F32, name="a", tag="act", bufs=4)
-            nc.scalar.activation(out=a[:], in_=vb[:], func=func)
-            return a
-
-        def back_r(bank, r):
-            cols = slice(BANK * bank, BANK * (bank + 1))
-            rh = work.tile([P, BANK], F32, name="rh", tag="prod", bufs=3)
-            nc.vector.tensor_tensor(out=rh[:], in0=r[:], in1=h_sb[:, cols], op=ALU.mult)
-            nc.vector.tensor_reduce(out=rhb[:, P * bank:P * (bank + 1)],
-                                    in_=rh[:].rearrange("p (n m) -> p n m", m=M), axis=AX.X, op=ALU.add)
-
-        def back_z(bank, z):
-            cols = slice(BANK * bank, BANK * (bank + 1))
-            nc.vector.scalar_tensor_tensor(out=neg_a[:, cols], in0=z[:], scalar=1.0, in1=h_sb[:, cols],
-                                           op0=ALU.subtract, op1=ALU.mult)
-            nc.gpsimd.tensor_tensor(out=za[:, cols], in0=z[:], in1=alpha_flat, op=ALU.mult)
-
-        def back_h(bank, hh):
-            cols = slice(BANK * bank, BANK * (bank + 1))
-            t1 = work.tile([P, BANK], F32, name="t1", tag="prod", bufs=3)
-            nc.vector.tensor_tensor(out=t1[:], in0=hh[:], in1=za[:, cols], op=ALU.mult)
-            hn = work.tile([P, BANK], F32, name="hn", tag="hn", bufs=4)
-            nc.vector.tensor_tensor(out=hn[:], in0=t1[:], in1=neg_a[:, cols], op=ALU.subtract)
-            queue = nc.gpsimd if bank < 6 else nc.sync
-            queue.dma_start(out=out_1[:, cols], in_=hn[:])
-            nc.vector.tensor_reduce(out=o0[:, P * bank:P * (bank + 1)],
-                                    in_=hn[:].rearrange("p (n m) -> p n m", m=M), axis=AX.X, op=ALU.add)
-            if bank == 3:
-                nc.gpsimd.dma_start(out=out_0[:, 0:512], in_=o0[:, 0:512])
-            elif bank == 5:
-                nc.gpsimd.dma_start(out=out_0[:, 512:768], in_=o0[:, 512:768])
-            elif bank >= 6:
-                nc.sync.dma_start(out=out_0[:, P * bank:P * (bank + 1)], in_=o0[:, P * bank:P * (bank + 1)])
-
-        backs = {"r": back_r, "z": back_z, "h": back_h}
         funcs = {"r": ACT.Sigmoid, "z": ACT.Sigmoid, "h": ACT.Tanh}
-        flips = {5: 0, 9: 1}
+        mx = {}
+        act = {}
+        pre = {}
+        back = {}
 
-        for i in range(len(chunks)):
-            passes(i)
-            if i + RING < len(chunks):
-                load(i + RING)
+        def passes(n):
+            w, kb, k, off, last = banks[n]
+            t = tiles[k]
+            mx[n] = psum.tile([P, 4, P], F32, name="mx%d" % n, tag="mx")
+            for c in range(4):
+                for g in range(4):
+                    if w == "h" and g >= 2:
+                        rw = codes_r[:, P * (g - 2):P * (g - 1)]
+                        rs = ascl_r[:, P * (g - 2):P * (g - 1)]
+                    else:
+                        rw = codes[:, P * g:P * (g + 1)]
+                        rs = ascl[:, P * g:P * (g + 1)]
+                    col = BANK * kb + P * c
+                    nc.tensor.matmul_mx(
+                        out=mx[n][:, c, :],
+                        lhsT=t[:, g, off + P * c:off + P * (c + 1)].bitcast(FP8X4),
+                        lhsT_scale=planes[w][4 * g:P, col:col + P],
+                        rhs=rw.bitcast(FP8X4), rhs_scale=rs,
+                        start=(g == 0), stop=(g == 3),
+                    )
+
+        def acts(n):
+            w, kb, k, off, last = banks[n]
+            j = order.index(w)
+            if w == "z":
+                dst = z_t[:, 4 * kb:4 * (kb + 1), :]
+            else:
+                act[n] = work.tile([P, 4, P], F32, name="a%d" % n, tag="act", bufs=3)
+                dst = act[n][:]
+            for c in range(4):
+                idx = 32 * j + 4 * kb + c
+                nc.scalar.activation(out=dst[:, c, :], in_=mx[n][:, c, :], func=funcs[w],
+                                     bias=bias_pp[:, idx:idx + 1], scale=1.0)
+
+        def first(n):
+            w, kb, k, off, last = banks[n]
+            sl = slice(4 * kb, 4 * (kb + 1))
+            if w == "r":
+                pre[n] = work.tile([P, 4, P], F32, name="rh%d" % n, tag="pre", bufs=4)
+                nc.vector.tensor_tensor(out=pre[n][:], in0=act[n][:], in1=h_t[:, sl, :], op=ALU.mult)
+            elif w == "z":
+                nc.vector.scalar_tensor_tensor(out=neg_a[:, sl, :], in0=z_t[:, sl, :], scalar=1.0, in1=h_t[:, sl, :],
+                                               op0=ALU.subtract, op1=ALU.mult)
+            else:
+                t1 = work.tile([P, 4, P], F32, name="t1", tag="t1", bufs=2)
+                nc.vector.scalar_tensor_tensor(out=t1[:], in0=act[n][:], scalar=alpha_pp[:, 0:1], in1=z_t[:, sl, :],
+                                               op0=ALU.mult, op1=ALU.mult)
+                pre[n] = work.tile([P, 4, P], F32, name="hn%d" % n, tag="pre", bufs=4)
+                nc.vector.tensor_tensor(out=pre[n][:], in0=t1[:], in1=neg_a[:, sl, :], op=ALU.subtract)
+
+        def flip_back(n):
+            back[n] = psum.tile([P, 4, P], F32, name="tb%d" % n, tag="tb")
+            for c in range(4):
+                nc.tensor.transpose(back[n][:, c, :], pre[n][:, c, :], ident_f[:])
+
+        def second(n):
+            w, kb, k, off, last = banks[n]
+            view = back[n][:].rearrange("p c (n m) -> p (c n) m", m=M)
+            if w == "r":
+                nc.vector.tensor_reduce(out=rhb[:, P * kb:P * (kb + 1)], in_=view, axis=AX.X, op=ALU.add)
+            else:
+                hn = work.tile([P, BANK], F32, name="hn", tag="hn", bufs=4)
+                nc.scalar.copy(out=hn[:], in_=back[n][:].rearrange("p c j -> p (c j)"))
+                queue = nc.gpsimd if kb < 6 else nc.sync
+                queue.dma_start(out=out_1[:, BANK * kb:BANK * (kb + 1)], in_=hn[:])
+                nc.vector.tensor_reduce(out=o0[:, P * kb:P * (kb + 1)], in_=view, axis=AX.X, op=ALU.add)
+                if kb == 3:
+                    nc.gpsimd.dma_start(out=out_0[:, 0:512], in_=o0[:, 0:512])
+                elif kb == 5:
+                    nc.gpsimd.dma_start(out=out_0[:, 512:768], in_=o0[:, 512:768])
+                elif kb >= 6:
+                    nc.sync.dma_start(out=out_0[:, P * kb:P * (kb + 1)], in_=o0[:, P * kb:P * (kb + 1)])
+
+        total = len(banks)
+        flips = {3 + LAG + 1: 0, 7 + LAG + 1: 1}
+        for n in range(total + LAG):
+            if n < total:
+                passes(n)
+                if banks[n][4] and banks[n][2] + RING < len(blocks):
+                    load(banks[n][2] + RING)
+            o = n - LAG
+            turn = o >= 0 and banks[o][0] != "z"
+            if turn:
+                flip_back(o)
             tp = None
-            if i in flips:
-                tp = flip_units(rhb, flips[i])
-            w = chunks[i][0]
-            closed = [bank for g, bank, off in chunks[i][4] if g == 3]
-            outs = [front(w, bank, funcs[w]) for bank in closed]
-            grp = None
-            if i in flips:
+            if n in flips:
+                tp = flip_units(rhb, flips[n])
+            if n < total:
+                acts(n)
+            if turn:
+                second(o)
+            if n in flips:
                 grp = group_units(nc.scalar.copy, tp)
-            if i == 1:
-                spread_bias("z")
-            if i == 4:
-                spread_bias("h")
-            for bank, a in zip(closed, outs):
-                backs[w](bank, a)
-            if i in flips:
-                half = flips[i]
+            if n < total:
+                first(n)
+            if n in flips:
+                half = flips[n]
                 quantise(grp, codes_r[:, P * half:P * (half + 1)], ascl_r[:, P * half:P * (half + 1)])

@@ -21,6 +21,7 @@ NM = UNITS * M
 BANK = 512
 RING = 6
 LAG = 2
+STORES = {3: 0, 5: 4, 6: 6, 7: 7}
 
 FLOPS = 2 * 128 * 2048 * 4096 * 3
 
@@ -38,17 +39,28 @@ def tile_ctgrucell_w_kernel(
     order = ("r", "z", "h")
 
     blocks = []
-    for w in ("r", "z"):
-        for j in range(4):
-            blocks.append((w, 1024 * j, 1024))
-    for j in range(3):
-        blocks.append(("h", 1024 * j, 1024))
-    blocks.append(("h", 3072, 512))
-    blocks.append(("h", 3584, 512))
     banks = []
-    for k, (w, c0, ncols) in enumerate(blocks):
+
+    def add_span(w, c0, ncols, split):
+        first_load = len(blocks)
+        if split:
+            blocks.append((w, 0, 2, c0, ncols))
+            blocks.append((w, 2, 2, c0, ncols))
+            where = {0: (first_load, 0), 1: (first_load, 1), 2: (first_load + 1, 0), 3: (first_load + 1, 1)}
+        else:
+            blocks.append((w, 0, 4, c0, ncols))
+            where = {0: (first_load, 0), 1: (first_load, 1), 2: (first_load, 2), 3: (first_load, 3)}
         for i in range(ncols // BANK):
-            banks.append((w, c0 // BANK + i, k, BANK * i, i == ncols // BANK - 1))
+            done = list(range(first_load, len(blocks))) if i == ncols // BANK - 1 else []
+            banks.append((w, c0 // BANK + i, where, BANK * i, done))
+
+    for w in ("r", "z"):
+        add_span(w, 0, 2048, True)
+        add_span(w, 2048, 2048, True)
+    add_span("h", 0, 2048, True)
+    add_span("h", 2048, 1024, False)
+    add_span("h", 3072, 512, False)
+    add_span("h", 3584, 512, False)
 
     with ExitStack() as ctx:
         ctx.enter_context(nc.allow_low_precision(reason="sums are made in float32 and rounded once to bfloat16"))
@@ -82,18 +94,18 @@ def tile_ctgrucell_w_kernel(
         tiles = {}
 
         def load(k):
-            w, c0, ncols = blocks[k]
+            w, g0, ng, c0, ncols = blocks[k]
             if k == 0:
                 load_scales("r")
-            elif k == 2:
+            elif k == 4:
                 load_scales("z")
-            elif k == 6:
+            elif k == 8:
                 load_scales("h")
-            t = ring.tile([P, 4, ncols], U32, name="w%d" % k, tag="w", align_bytes=64)
+            t = ring.tile([P, ng, ncols], U32, name="w%d" % k, tag="w", align_bytes=64)
             tiles[k] = t
             nc.sync.dma_start(
                 out=t[:].bitcast(I32),
-                in_=words[w].rearrange("g p n t -> p g (n t)")[:, :, 4 * c0:4 * (c0 + ncols)].bitcast(I32),
+                in_=words[w].rearrange("g p n t -> p g (n t)")[:, g0:g0 + ng, 4 * c0:4 * (c0 + ncols)].bitcast(I32),
             )
 
         for k in range(RING):
@@ -124,6 +136,7 @@ def tile_ctgrucell_w_kernel(
         hs = keep.tile([P, UNITS], BF16, name="hs")
         rhb = keep.tile([P, UNITS], BF16, name="rhb")
         o0 = keep.tile([P, UNITS], F32, name="o0")
+        hn_all = keep.tile([P, NM], F32, name="hn_all")
 
         def flip_units(src, half):
             tp = psum.tile([P, 4, P], BF16, name="tp", tag="aux", bufs=2)
@@ -182,8 +195,7 @@ def tile_ctgrucell_w_kernel(
         back = {}
 
         def passes(n):
-            w, kb, k, off, last = banks[n]
-            t = tiles[k]
+            w, kb, where, off, done = banks[n]
             mx[n] = psum.tile([P, 4, P], F32, name="mx%d" % n, tag="mx")
             for c in range(4):
                 for g in range(4):
@@ -196,14 +208,14 @@ def tile_ctgrucell_w_kernel(
                     col = BANK * kb + P * c
                     nc.tensor.matmul_mx(
                         out=mx[n][:, c, :],
-                        lhsT=t[:, g, off + P * c:off + P * (c + 1)].bitcast(FP8X4),
+                        lhsT=tiles[where[g][0]][:, where[g][1], off + P * c:off + P * (c + 1)].bitcast(FP8X4),
                         lhsT_scale=planes[w][4 * g:P, col:col + P],
                         rhs=rw.bitcast(FP8X4), rhs_scale=rs,
                         start=(g == 0), stop=(g == 3),
                     )
 
         def acts(n):
-            w, kb, k, off, last = banks[n]
+            w, kb, where, off, done = banks[n]
             j = order.index(w)
             if w == "z":
                 dst = z_t[:, 4 * kb:4 * (kb + 1), :]
@@ -216,7 +228,7 @@ def tile_ctgrucell_w_kernel(
                                      bias=bias_pp[:, idx:idx + 1], scale=1.0)
 
         def first(n):
-            w, kb, k, off, last = banks[n]
+            w, kb, where, off, done = banks[n]
             sl = slice(4 * kb, 4 * (kb + 1))
             if w == "r":
                 pre[n] = work.tile([P, 4, P], F32, name="rh%d" % n, tag="pre", bufs=4)
@@ -237,30 +249,29 @@ def tile_ctgrucell_w_kernel(
                 nc.tensor.transpose(back[n][:, c, :], pre[n][:, c, :], ident_f[:])
 
         def second(n):
-            w, kb, k, off, last = banks[n]
+            w, kb, where, off, done = banks[n]
             view = back[n][:].rearrange("p c (n m) -> p (c n) m", m=M)
             if w == "r":
                 nc.vector.tensor_reduce(out=rhb[:, P * kb:P * (kb + 1)], in_=view, axis=AX.X, op=ALU.add)
             else:
-                hn = work.tile([P, BANK], F32, name="hn", tag="hn", bufs=4)
-                nc.scalar.copy(out=hn[:], in_=back[n][:].rearrange("p c j -> p (c j)"))
-                queue = nc.gpsimd if kb < 6 else nc.sync
-                queue.dma_start(out=out_1[:, BANK * kb:BANK * (kb + 1)], in_=hn[:])
+                nc.scalar.copy(out=hn_all[:, BANK * kb:BANK * (kb + 1)], in_=back[n][:].rearrange("p c j -> p (c j)"))
+                if kb in STORES:
+                    lo = BANK * STORES[kb]
+                    nc.sync.dma_start(out=out_1[:, lo:BANK * (kb + 1)], in_=hn_all[:, lo:BANK * (kb + 1)])
                 nc.vector.tensor_reduce(out=o0[:, P * kb:P * (kb + 1)], in_=view, axis=AX.X, op=ALU.add)
-                if kb == 3:
-                    nc.gpsimd.dma_start(out=out_0[:, 0:512], in_=o0[:, 0:512])
-                elif kb == 5:
-                    nc.gpsimd.dma_start(out=out_0[:, 512:768], in_=o0[:, 512:768])
-                elif kb >= 6:
-                    nc.sync.dma_start(out=out_0[:, P * kb:P * (kb + 1)], in_=o0[:, P * kb:P * (kb + 1)])
+                if kb == 5:
+                    nc.sync.dma_start(out=out_0[:, 0:768], in_=o0[:, 0:768])
+                elif kb == 7:
+                    nc.sync.dma_start(out=out_0[:, 768:1024], in_=o0[:, 768:1024])
 
         total = len(banks)
         flips = {3 + LAG + 1: 0, 7 + LAG + 1: 1}
         for n in range(total + LAG):
             if n < total:
                 passes(n)
-                if banks[n][4] and banks[n][2] + RING < len(blocks):
-                    load(banks[n][2] + RING)
+                for k in banks[n][4]:
+                    if k + RING < len(blocks):
+                        load(k + RING)
             o = n - LAG
             turn = o >= 0 and banks[o][0] != "z"
             if turn:

@@ -21,7 +21,6 @@ NM = UNITS * M
 BANK = 512
 RING = 6
 LAG = 2
-STORES = {3: 0, 5: 4, 6: 6, 7: 7}
 
 FLOPS = 2 * 128 * 2048 * 4096 * 3
 
@@ -39,10 +38,13 @@ def tile_ctgrucell_w_kernel(
     order = ("r", "z", "h")
 
     blocks = []
-    banks = []
+    units = []
+    first_block = {}
 
-    def add_span(w, c0, ncols, split):
+    def add_span(w, c0, ncols, split, piece):
         first_load = len(blocks)
+        if w not in first_block:
+            first_block[w] = first_load
         if split:
             blocks.append((w, 0, 2, c0, ncols))
             blocks.append((w, 2, 2, c0, ncols))
@@ -50,17 +52,19 @@ def tile_ctgrucell_w_kernel(
         else:
             blocks.append((w, 0, 4, c0, ncols))
             where = {0: (first_load, 0), 1: (first_load, 1), 2: (first_load, 2), 3: (first_load, 3)}
-        for i in range(ncols // BANK):
-            done = list(range(first_load, len(blocks))) if i == ncols // BANK - 1 else []
-            banks.append((w, c0 // BANK + i, where, BANK * i, done))
+        for i in range(ncols // piece):
+            last = i == ncols // piece - 1
+            done = list(range(first_load, len(blocks))) if last else []
+            units.append((w, (c0 + piece * i) // P, piece // P, where, piece * i, done, (c0, c0 + ncols) if last else None))
 
-    for w in ("r", "z"):
-        add_span(w, 0, 2048, True)
-        add_span(w, 2048, 2048, True)
-    add_span("h", 0, 2048, True)
-    add_span("h", 2048, 1024, False)
-    add_span("h", 3072, 512, False)
-    add_span("h", 3584, 512, False)
+    add_span("r", 0, 2048, True, BANK)
+    add_span("r", 2048, 2048, True, BANK)
+    add_span("z", 0, 2048, True, BANK)
+    add_span("h", 0, 2048, True, BANK)
+    add_span("z", 2048, 2048, True, BANK)
+    add_span("h", 2048, 1024, False, BANK)
+    add_span("h", 3072, 512, False, BANK)
+    add_span("h", 3584, 512, False, 256)
 
     with ExitStack() as ctx:
         ctx.enter_context(nc.allow_low_precision(reason="sums are made in float32 and rounded once to bfloat16"))
@@ -78,29 +82,21 @@ def tile_ctgrucell_w_kernel(
 
         def load_scales(w):
             for q in range(4):
-                nc.sync.dma_start(
-                    out=planes[w][32 * q:32 * q + 16, :].bitcast(I32),
-                    in_=scales[w][:, 4 * q:4 * q + 4, :].bitcast(I32),
-                )
+                for r in range(4):
+                    nc.gpsimd.dma_start(
+                        out=planes[w][32 * q + r:32 * q + 16:4, :].bitcast(F32),
+                        in_=scales[w][:, 4 * q + r, :].bitcast(F32),
+                    )
 
         x_sb = keep.tile([P, I_IN], BF16, name="x_sb")
         nc.scalar.dma_start(out=x_sb[:], in_=inputs)
         h_sb = keep.tile([P, NM], BF16, name="h_sb")
-        for half in range(2):
-            nc.scalar.dma_start(out=h_sb[:, 2048 * half:2048 * (half + 1)], in_=state[:, 2048 * half:2048 * (half + 1)])
-        for j, w in enumerate(order):
-            nc.scalar.dma_start(out=bsrc[32 * j:32 * (j + 1), :], in_=biases[w].rearrange("(c p) -> c p", p=P))
+        nc.scalar.dma_start(out=h_sb[:], in_=state)
 
         tiles = {}
 
         def load(k):
             w, g0, ng, c0, ncols = blocks[k]
-            if k == 0:
-                load_scales("r")
-            elif k == 4:
-                load_scales("z")
-            elif k == 8:
-                load_scales("h")
             t = ring.tile([P, ng, ncols], U32, name="w%d" % k, tag="w", align_bytes=64)
             tiles[k] = t
             nc.sync.dma_start(
@@ -121,6 +117,10 @@ def tile_ctgrucell_w_kernel(
         for m in range(M):
             nc.gpsimd.tensor_scalar(out=alpha_row[:, :, m], in0=ones[:], scalar1=alpha[m], scalar2=0.0,
                                     op0=ALU.mult, op1=ALU.add)
+        for j, w in enumerate(order):
+            nc.gpsimd.dma_start(out=bsrc[32 * j:32 * (j + 1), :], in_=biases[w].rearrange("(c p) -> c p", p=P))
+        for w in order:
+            load_scales(w)
         warm = keep.tile([P, 1], F32, name="warm")
         nc.scalar.activation(out=warm[:], in_=ones[:, 0:1], func=ACT.Sigmoid)
 
@@ -152,9 +152,8 @@ def tile_ctgrucell_w_kernel(
         def quantise(grp, c_out, s_out):
             nc.vector.quantize_mx(out=c_out.bitcast(FP8X4), scales=s_out, in_=grp[:])
 
-        def sum_state(half):
-            nc.vector.tensor_reduce(out=hs[:, 512 * half:512 * (half + 1)],
-                                    in_=h_sb[:, 2048 * half:2048 * (half + 1)].rearrange("p (n m) -> p n m", m=M),
+        def sum_scales(dst, src, lo, hi):
+            nc.vector.tensor_reduce(out=dst[:, lo // M:hi // M], in_=src[:, lo:hi].rearrange("p (n m) -> p n m", m=M),
                                     axis=AX.X, op=ALU.add)
 
         xw = x_sb[:].bitcast(F32)
@@ -167,10 +166,10 @@ def tile_ctgrucell_w_kernel(
             out=gx[:].bitcast(F32).rearrange("p (g b u) -> p g b u", g=2, u=2),
             in_=tpx[:].rearrange("p g u b -> p g b u"),
         )
-        sum_state(0)
+        sum_scales(hs, h_sb, 0, 2048)
         nc.vector.quantize_mx(out=codes[:, 0:256].bitcast(FP8X4), scales=ascl[:, 0:256], in_=gx[:])
         tp0 = flip_units(hs, 0)
-        sum_state(1)
+        sum_scales(hs, h_sb, 2048, 4096)
         grp0 = group_units(nc.vector.tensor_copy, tp0)
         tp1 = flip_units(hs, 1)
         grp1 = group_units(nc.vector.tensor_copy, tp1)
@@ -195,9 +194,9 @@ def tile_ctgrucell_w_kernel(
         back = {}
 
         def passes(n):
-            w, kb, where, off, done = banks[n]
-            mx[n] = psum.tile([P, 4, P], F32, name="mx%d" % n, tag="mx")
-            for c in range(4):
+            w, cc, nch, where, off, done, span = units[n]
+            mx[n] = psum.tile([P, nch, P], F32, name="mx%d" % n, tag="mx")
+            for c in range(nch):
                 for g in range(4):
                     if w == "h" and g >= 2:
                         rw = codes_r[:, P * (g - 2):P * (g - 1)]
@@ -205,7 +204,7 @@ def tile_ctgrucell_w_kernel(
                     else:
                         rw = codes[:, P * g:P * (g + 1)]
                         rs = ascl[:, P * g:P * (g + 1)]
-                    col = BANK * kb + P * c
+                    col = P * (cc + c)
                     nc.tensor.matmul_mx(
                         out=mx[n][:, c, :],
                         lhsT=tiles[where[g][0]][:, where[g][1], off + P * c:off + P * (c + 1)].bitcast(FP8X4),
@@ -215,65 +214,71 @@ def tile_ctgrucell_w_kernel(
                     )
 
         def acts(n):
-            w, kb, where, off, done = banks[n]
+            w, cc, nch, where, off, done, span = units[n]
             j = order.index(w)
             if w == "z":
-                dst = z_t[:, 4 * kb:4 * (kb + 1), :]
+                dst = z_t[:, cc:cc + nch, :]
             else:
-                act[n] = work.tile([P, 4, P], F32, name="a%d" % n, tag="act", bufs=3)
+                act[n] = work.tile([P, nch, P], F32, name="a%d" % n, tag="act", bufs=3)
                 dst = act[n][:]
-            for c in range(4):
-                idx = 32 * j + 4 * kb + c
+            for c in range(nch):
+                idx = 32 * j + cc + c
                 nc.scalar.activation(out=dst[:, c, :], in_=mx[n][:, c, :], func=funcs[w],
                                      bias=bias_pp[:, idx:idx + 1], scale=1.0)
 
         def first(n):
-            w, kb, where, off, done = banks[n]
-            sl = slice(4 * kb, 4 * (kb + 1))
+            w, cc, nch, where, off, done, span = units[n]
+            sl = slice(cc, cc + nch)
             if w == "r":
-                pre[n] = work.tile([P, 4, P], F32, name="rh%d" % n, tag="pre", bufs=4)
+                pre[n] = work.tile([P, nch, P], F32, name="rh%d" % n, tag="pre", bufs=4)
                 nc.vector.tensor_tensor(out=pre[n][:], in0=act[n][:], in1=h_t[:, sl, :], op=ALU.mult)
             elif w == "z":
                 nc.vector.scalar_tensor_tensor(out=neg_a[:, sl, :], in0=z_t[:, sl, :], scalar=1.0, in1=h_t[:, sl, :],
                                                op0=ALU.subtract, op1=ALU.mult)
             else:
-                t1 = work.tile([P, 4, P], F32, name="t1", tag="t1", bufs=2)
+                t1 = work.tile([P, nch, P], F32, name="t1", tag="t1", bufs=2)
                 nc.vector.scalar_tensor_tensor(out=t1[:], in0=act[n][:], scalar=alpha_pp[:, 0:1], in1=z_t[:, sl, :],
                                                op0=ALU.mult, op1=ALU.mult)
-                pre[n] = work.tile([P, 4, P], F32, name="hn%d" % n, tag="pre", bufs=4)
+                pre[n] = work.tile([P, nch, P], F32, name="hn%d" % n, tag="pre", bufs=4)
                 nc.vector.tensor_tensor(out=pre[n][:], in0=t1[:], in1=neg_a[:, sl, :], op=ALU.subtract)
 
         def flip_back(n):
-            back[n] = psum.tile([P, 4, P], F32, name="tb%d" % n, tag="tb")
-            for c in range(4):
+            nch = units[n][2]
+            back[n] = psum.tile([P, nch, P], F32, name="tb%d" % n, tag="tb")
+            for c in range(nch):
                 nc.tensor.transpose(back[n][:, c, :], pre[n][:, c, :], ident_f[:])
 
-        def second(n):
-            w, kb, where, off, done = banks[n]
-            view = back[n][:].rearrange("p c (n m) -> p (c n) m", m=M)
-            if w == "r":
-                nc.vector.tensor_reduce(out=rhb[:, P * kb:P * (kb + 1)], in_=view, axis=AX.X, op=ALU.add)
-            else:
-                nc.scalar.copy(out=hn_all[:, BANK * kb:BANK * (kb + 1)], in_=back[n][:].rearrange("p c j -> p (c j)"))
-                if kb in STORES:
-                    lo = BANK * STORES[kb]
-                    nc.sync.dma_start(out=out_1[:, lo:BANK * (kb + 1)], in_=hn_all[:, lo:BANK * (kb + 1)])
-                nc.vector.tensor_reduce(out=o0[:, P * kb:P * (kb + 1)], in_=view, axis=AX.X, op=ALU.add)
-                if kb == 5:
-                    nc.sync.dma_start(out=out_0[:, 0:768], in_=o0[:, 0:768])
-                elif kb == 7:
-                    nc.sync.dma_start(out=out_0[:, 768:1024], in_=o0[:, 768:1024])
+        sums = []
 
-        total = len(banks)
+        def second(n):
+            w, cc, nch, where, off, done, span = units[n]
+            if w == "r":
+                nc.vector.tensor_reduce(out=rhb[:, 32 * cc:32 * (cc + nch)],
+                                        in_=back[n][:].rearrange("p c (n m) -> p (c n) m", m=M), axis=AX.X, op=ALU.add)
+            else:
+                nc.scalar.copy(out=hn_all[:, P * cc:P * (cc + nch)], in_=back[n][:].rearrange("p c j -> p (c j)"))
+                if span is not None:
+                    nc.sync.dma_start(out=out_1[:, span[0]:span[1]], in_=hn_all[:, span[0]:span[1]])
+                    sums.append(span)
+
+        def third():
+            lo, hi = sums.pop(0)
+            sum_scales(o0, hn_all, lo, hi)
+            if hi == 3072:
+                nc.sync.dma_start(out=out_0[:, 0:768], in_=o0[:, 0:768])
+            elif hi == 4096:
+                nc.sync.dma_start(out=out_0[:, 768:1024], in_=o0[:, 768:1024])
+
+        total = len(units)
         flips = {3 + LAG + 1: 0, 7 + LAG + 1: 1}
         for n in range(total + LAG):
             if n < total:
                 passes(n)
-                for k in banks[n][4]:
+                for k in units[n][5]:
                     if k + RING < len(blocks):
                         load(k + RING)
             o = n - LAG
-            turn = o >= 0 and banks[o][0] != "z"
+            turn = o >= 0 and units[o][0] != "z"
             if turn:
                 flip_back(o)
             tp = None
@@ -281,6 +286,7 @@ def tile_ctgrucell_w_kernel(
                 tp = flip_units(rhb, flips[n])
             if n < total:
                 acts(n)
+            waiting = len(sums) > 0
             if turn:
                 second(o)
             if n in flips:
@@ -290,3 +296,7 @@ def tile_ctgrucell_w_kernel(
             if n in flips:
                 half = flips[n]
                 quantise(grp, codes_r[:, P * half:P * (half + 1)], ascl_r[:, P * half:P * (half + 1)])
+            if waiting:
+                third()
+        while len(sums) > 0:
+            third()

@@ -82,11 +82,10 @@ def tile_ctgrucell_w_kernel(
 
         def load_scales(w):
             for q in range(4):
-                for r in range(4):
-                    nc.gpsimd.dma_start(
-                        out=planes[w][32 * q + r:32 * q + 16:4, :].bitcast(F32),
-                        in_=scales[w][:, 4 * q + r, :].bitcast(F32),
-                    )
+                nc.gpsimd.dma_start(
+                    out=planes[w][32 * q:32 * q + 16, :].bitcast(F32),
+                    in_=scales[w][:, 4 * q:4 * q + 4, :].bitcast(F32),
+                )
 
         x_sb = keep.tile([P, I_IN], BF16, name="x_sb")
         nc.scalar.dma_start(out=x_sb[:], in_=inputs)

@@ -61,10 +61,12 @@ def tile_ctgrucell_w_kernel(
     add_span("r", 2048, 2048, True, BANK)
     add_span("z", 0, 2048, True, BANK)
     add_span("h", 0, 2048, True, BANK)
-    add_span("z", 2048, 2048, True, BANK)
+    add_span("z", 2048, 1024, False, BANK)
+    add_span("z", 3072, 1024, False, BANK)
     add_span("h", 2048, 1024, False, BANK)
     add_span("h", 3072, 512, False, BANK)
-    add_span("h", 3584, 512, False, 256)
+    add_span("h", 3584, 256, False, 256)
+    add_span("h", 3840, 256, False, 256)
 
     with ExitStack() as ctx:
         ctx.enter_context(nc.allow_low_precision(reason="sums are made in float32 and rounded once to bfloat16"))
@@ -82,9 +84,9 @@ def tile_ctgrucell_w_kernel(
 
         def load_scales(w):
             for q in range(4):
-                nc.gpsimd.dma_start(
-                    out=planes[w][32 * q:32 * q + 16, :].bitcast(F32),
-                    in_=scales[w][:, 4 * q:4 * q + 4, :].bitcast(F32),
+                nc.sync.dma_start(
+                    out=planes[w][32 * q:32 * q + 16, :].bitcast(I32),
+                    in_=scales[w][:, 4 * q:4 * q + 4, :].bitcast(I32),
                 )
 
         x_sb = keep.tile([P, I_IN], BF16, name="x_sb")
@@ -103,6 +105,8 @@ def tile_ctgrucell_w_kernel(
                 in_=words[w].rearrange("g p n t -> p g (n t)")[:, g0:g0 + ng, 4 * c0:4 * (c0 + ncols)].bitcast(I32),
             )
 
+        for w in order:
+            load_scales(w)
         for k in range(RING):
             load(k)
 
@@ -118,8 +122,6 @@ def tile_ctgrucell_w_kernel(
                                     op0=ALU.mult, op1=ALU.add)
         for j, w in enumerate(order):
             nc.gpsimd.dma_start(out=bsrc[32 * j:32 * (j + 1), :], in_=biases[w].rearrange("(c p) -> c p", p=P))
-        for w in order:
-            load_scales(w)
         warm = keep.tile([P, 1], F32, name="warm")
         nc.scalar.activation(out=warm[:], in_=ones[:, 0:1], func=ACT.Sigmoid)
 
@@ -247,8 +249,6 @@ def tile_ctgrucell_w_kernel(
             for c in range(nch):
                 nc.tensor.transpose(back[n][:, c, :], pre[n][:, c, :], ident_f[:])
 
-        sums = []
-
         def second(n):
             w, cc, nch, where, off, done, span = units[n]
             if w == "r":
@@ -258,11 +258,12 @@ def tile_ctgrucell_w_kernel(
                 nc.scalar.copy(out=hn_all[:, P * cc:P * (cc + nch)], in_=back[n][:].rearrange("p c j -> p (c j)"))
                 if span is not None:
                     nc.sync.dma_start(out=out_1[:, span[0]:span[1]], in_=hn_all[:, span[0]:span[1]])
-                    sums.append(span)
 
-        def third():
-            lo, hi = sums.pop(0)
-            sum_scales(o0, hn_all, lo, hi)
+        def third(n):
+            cc, nch = units[n][1], units[n][2]
+            nc.vector.tensor_reduce(out=o0[:, 32 * cc:32 * (cc + nch)],
+                                    in_=back[n][:].rearrange("p c (n m) -> p (c n) m", m=M), axis=AX.X, op=ALU.add)
+            hi = P * (cc + nch)
             if hi == 3072:
                 nc.sync.dma_start(out=out_0[:, 0:768], in_=o0[:, 0:768])
             elif hi == 4096:
@@ -285,7 +286,6 @@ def tile_ctgrucell_w_kernel(
                 tp = flip_units(rhb, flips[n])
             if n < total:
                 acts(n)
-            waiting = len(sums) > 0
             if turn:
                 second(o)
             if n in flips:
@@ -295,7 +295,5 @@ def tile_ctgrucell_w_kernel(
             if n in flips:
                 half = flips[n]
                 quantise(grp, codes_r[:, P * half:P * (half + 1)], ascl_r[:, P * half:P * (half + 1)])
-            if waiting:
-                third()
-        while len(sums) > 0:
-            third()
+            if turn and units[o][0] == "h":
+                third(o)

@@ -84,9 +84,9 @@ def tile_ctgrucell_w_kernel(
 
         def load_scales(w):
             for q in range(4):
-                nc.sync.dma_start(
-                    out=planes[w][32 * q:32 * q + 16, :].bitcast(I32),
-                    in_=scales[w][:, 4 * q:4 * q + 4, :].bitcast(I32),
+                nc.gpsimd.dma_start(
+                    out=planes[w][32 * q:32 * q + 16, :].bitcast(F32),
+                    in_=scales[w][:, 4 * q:4 * q + 4, :].bitcast(F32),
                 )
 
         x_sb = keep.tile([P, I_IN], BF16, name="x_sb")
@@ -105,8 +105,6 @@ def tile_ctgrucell_w_kernel(
                 in_=words[w].rearrange("g p n t -> p g (n t)")[:, g0:g0 + ng, 4 * c0:4 * (c0 + ncols)].bitcast(I32),
             )
 
-        for w in order:
-            load_scales(w)
         for k in range(RING):
             load(k)
 
@@ -122,6 +120,8 @@ def tile_ctgrucell_w_kernel(
                                     op0=ALU.mult, op1=ALU.add)
         for j, w in enumerate(order):
             nc.gpsimd.dma_start(out=bsrc[32 * j:32 * (j + 1), :], in_=biases[w].rearrange("(c p) -> c p", p=P))
+        for w in order:
+            load_scales(w)
         warm = keep.tile([P, 1], F32, name="warm")
         nc.scalar.activation(out=warm[:], in_=ones[:, 0:1], func=ACT.Sigmoid)
 

from contextlib import ExitStack

import concourse.mybir as mybir
from concourse.masks import make_identity

F32 = mybir.dt.float32
BF16 = mybir.dt.bfloat16
I32 = mybir.dt.int32
U32 = mybir.dt.uint32
U8 = mybir.dt.uint8
FP8X4 = mybir.dt.float8_e4m3fn_x4
ALU = mybir.AluOpType
ACT = mybir.ActivationFunctionType
AX = mybir.AxisListType

P = 128
I_IN = 1024
UNITS = 1024
M = 4
NM = UNITS * M
BANK = 512
RING = 6
LAG = 2

FLOPS = 2 * 128 * 2048 * 4096 * 3


def tile_ctgrucell_w_kernel(
    tc, inputs, state, W_z_words, W_z_scales, b_z, W_r_words, W_r_scales, b_r,
    W_h_words, W_h_scales, b_h, out_0, out_1,
):
    nc = tc.nc
    raw = [10.0 ** (-0.5 * m) for m in range(M)]
    alpha = [v / sum(raw) for v in raw]
    words = {"r": W_r_words, "z": W_z_words, "h": W_h_words}
    scales = {"r": W_r_scales, "z": W_z_scales, "h": W_h_scales}
    biases = {"r": b_r, "z": b_z, "h": b_h}
    order = ("r", "z", "h")

    blocks = []
    units = []
    first_block = {}

    def add_span(w, c0, ncols, split, piece):
        first_load = len(blocks)
        if w not in first_block:
            first_block[w] = first_load
        if split:
            blocks.append((w, 0, 2, c0, ncols))
            blocks.append((w, 2, 2, c0, ncols))
            where = {0: (first_load, 0), 1: (first_load, 1), 2: (first_load + 1, 0), 3: (first_load + 1, 1)}
        else:
            blocks.append((w, 0, 4, c0, ncols))
            where = {0: (first_load, 0), 1: (first_load, 1), 2: (first_load, 2), 3: (first_load, 3)}
        for i in range(ncols // piece):
            last = i == ncols // piece - 1
            done = list(range(first_load, len(blocks))) if last else []
            units.append((w, (c0 + piece * i) // P, piece // P, where, piece * i, done, (c0, c0 + ncols) if last else None))

    add_span("r", 0, 2048, True, BANK)
    add_span("r", 2048, 2048, True, BANK)
    add_span("z", 0, 2048, True, BANK)
    add_span("h", 0, 2048, True, BANK)
    add_span("z", 2048, 1024, False, BANK)
    add_span("z", 3072, 1024, False, BANK)
    add_span("h", 2048, 1024, False, BANK)
    add_span("h", 3072, 512, False, BANK)
    add_span("h", 3584, 256, False, 256)
    add_span("h", 3840, 256, False, 256)

    with ExitStack() as ctx:
        ctx.enter_context(nc.allow_low_precision(reason="sums are made in float32 and rounded once to bfloat16"))
        keep = ctx.enter_context(tc.tile_pool(name="keep", bufs=1))
        ring = ctx.enter_context(tc.tile_pool(name="ring", bufs=RING))
        work = ctx.enter_context(tc.tile_pool(name="work", bufs=3))
        psum = ctx.enter_context(tc.psum_pool(name="psum", bufs=3))

        planes = {}
        for w in order:
            planes[w] = keep.tile([P, NM], U8, name="planes_" + w, align_bytes=64)
            nc.vector.memset(planes[w][:].bitcast(I32), 0)
        bsrc = keep.tile([P, P], BF16, name="bsrc")
        nc.vector.memset(bsrc[:], 0.0)

        def load_scales(w):
            for q in range(4):
                nc.gpsimd.dma_start(
                    out=planes[w][32 * q:32 * q + 16, :].bitcast(F32),
                    in_=scales[w][:, 4 * q:4 * q + 4, :].bitcast(F32),
                )

        x_sb = keep.tile([P, I_IN], BF16, name="x_sb")
        nc.scalar.dma_start(out=x_sb[:], in_=inputs)
        h_sb = keep.tile([P, NM], BF16, name="h_sb")
        nc.scalar.dma_start(out=h_sb[:], in_=state)

        tiles = {}

        def load(k):
            w, g0, ng, c0, ncols = blocks[k]
            t = ring.tile([P, ng, ncols], U32, name="w%d" % k, tag="w", align_bytes=64)
            tiles[k] = t
            nc.sync.dma_start(
                out=t[:].bitcast(I32),
                in_=words[w].rearrange("g p n t -> p g (n t)")[:, g0:g0 + ng, 4 * c0:4 * (c0 + ncols)].bitcast(I32),
            )

        for k in range(RING):
            load(k)

        ident_f = keep.tile([P, P], F32, name="ident_f")
        make_identity(nc, ident_f[:])
        ident_b = keep.tile([P, P], BF16, name="ident_b")
        make_identity(nc, ident_b[:])
        ones = keep.tile([P, 32], F32, name="ones")
        nc.gpsimd.memset(ones[:], 1.0)
        alpha_row = keep.tile([P, 32, M], F32, name="alpha_row")
        for m in range(M):
            nc.gpsimd.tensor_scalar(out=alpha_row[:, :, m], in0=ones[:], scalar1=alpha[m], scalar2=0.0,
                                    op0=ALU.mult, op1=ALU.add)
        for j, w in enumerate(order):
            nc.gpsimd.dma_start(out=bsrc[32 * j:32 * (j + 1), :], in_=biases[w].rearrange("(c p) -> c p", p=P))
        for w in order:
            load_scales(w)
        warm = keep.tile([P, 1], F32, name="warm")
        nc.scalar.activation(out=warm[:], in_=ones[:, 0:1], func=ACT.Sigmoid)

        codes = keep.tile([P, 4 * P], U32, name="codes", align_bytes=64)
        ascl = keep.tile([P, 4 * P], U8, name="ascl", align_bytes=64)
        codes_r = keep.tile([P, 2 * P], U32, name="codes_r", align_bytes=64)
        ascl_r = keep.tile([P, 2 * P], U8, name="ascl_r", align_bytes=64)
        bias_pp = keep.tile([P, P], F32, name="bias_pp")
        alpha_pp = keep.tile([P, 1], F32, name="alpha_pp")
        h_t = keep.tile([P, 32, P], BF16, name="h_t")
        z_t = keep.tile([P, 32, P], F32, name="z_t")
        neg_a = keep.tile([P, 32, P], F32, name="neg_a")
        hs = keep.tile([P, UNITS], BF16, name="hs")
        rhb = keep.tile([P, UNITS], BF16, name="rhb")
        o0 = keep.tile([P, UNITS], F32, name="o0")
        hn_all = keep.tile([P, NM], F32, name="hn_all")

        def flip_units(src, half):
            tp = psum.tile([P, 4, P], BF16, name="tp", tag="aux", bufs=2)
            for t in range(4):
                nc.tensor.transpose(tp[:, t, :], src[:, 512 * half + t:512 * (half + 1):4], ident_b[:])
            return tp

        def group_units(engine_copy, tp):
            grp = work.tile([P, BANK], BF16, name="grp", tag="grp", bufs=2, align_bytes=64)
            engine_copy(out=grp[:].rearrange("p (b t) -> p b t", t=4), in_=tp[:].rearrange("p t b -> p b t"))
            return grp

        def quantise(grp, c_out, s_out):
            nc.vector.quantize_mx(out=c_out.bitcast(FP8X4), scales=s_out, in_=grp[:])

        def sum_scales(dst, src, lo, hi):
            nc.vector.tensor_reduce(out=dst[:, lo // M:hi // M], in_=src[:, lo:hi].rearrange("p (n m) -> p n m", m=M),
                                    axis=AX.X, op=ALU.add)

        xw = x_sb[:].bitcast(F32)
        tpx = psum.tile([P, 2, 2, P], F32, name="tpx", tag="aux", bufs=2)
        for g in range(2):
            for u in range(2):
                nc.tensor.transpose(tpx[:, g, u, :], xw[:, 256 * g + u:256 * (g + 1):2], ident_f[:])
        gx = keep.tile([P, 1024], BF16, name="gx", align_bytes=64)
        nc.vector.tensor_copy(
            out=gx[:].bitcast(F32).rearrange("p (g b u) -> p g b u", g=2, u=2),
            in_=tpx[:].rearrange("p g u b -> p g b u"),
        )
        sum_scales(hs, h_sb, 0, 2048)
        nc.vector.quantize_mx(out=codes[:, 0:256].bitcast(FP8X4), scales=ascl[:, 0:256], in_=gx[:])
        tp0 = flip_units(hs, 0)
        sum_scales(hs, h_sb, 2048, 4096)
        grp0 = group_units(nc.vector.tensor_copy, tp0)
        tp1 = flip_units(hs, 1)
        grp1 = group_units(nc.vector.tensor_copy, tp1)
        quantise(grp0, codes[:, 256:384], ascl[:, 256:384])
        quantise(grp1, codes[:, 384:512], ascl[:, 384:512])
        tpb = psum.tile([P, P], BF16, name="tpb", tag="tb")
        nc.tensor.transpose(tpb[:], bsrc[:], ident_b[:])
        nc.scalar.copy(out=bias_pp[:], in_=tpb[:])
        tpa = psum.tile([P, P], F32, name="tpa", tag="tb")
        nc.tensor.transpose(tpa[:], alpha_row[:].rearrange("p n m -> p (n m)"), ident_f[:])
        nc.scalar.copy(out=alpha_pp[:], in_=tpa[:, 0:1])
        for q in range(4):
            tph = psum.tile([P, 8, P], BF16, name="tph", tag="tb")
            for c in range(8):
                nc.tensor.transpose(tph[:, c, :], h_sb[:, P * (8 * q + c):P * (8 * q + c + 1)], ident_b[:])
            nc.scalar.copy(out=h_t[:, 8 * q:8 * (q + 1), :], in_=tph[:])

        funcs = {"r": ACT.Sigmoid, "z": ACT.Sigmoid, "h": ACT.Tanh}
        mx = {}
        act = {}
        pre = {}
        back = {}

        def passes(n):
            w, cc, nch, where, off, done, span = units[n]
            mx[n] = psum.tile([P, nch, P], F32, name="mx%d" % n, tag="mx")
            for c in range(nch):
                for g in range(4):
                    if w == "h" and g >= 2:
                        rw = codes_r[:, P * (g - 2):P * (g - 1)]
                        rs = ascl_r[:, P * (g - 2):P * (g - 1)]
                    else:
                        rw = codes[:, P * g:P * (g + 1)]
                        rs = ascl[:, P * g:P * (g + 1)]
                    col = P * (cc + c)
                    nc.tensor.matmul_mx(
                        out=mx[n][:, c, :],
                        lhsT=tiles[where[g][0]][:, where[g][1], off + P * c:off + P * (c + 1)].bitcast(FP8X4),
                        lhsT_scale=planes[w][4 * g:P, col:col + P],
                        rhs=rw.bitcast(FP8X4), rhs_scale=rs,
                        start=(g == 0), stop=(g == 3),
                    )

        def acts(n):
            w, cc, nch, where, off, done, span = units[n]
            j = order.index(w)
            if w == "z":
                dst = z_t[:, cc:cc + nch, :]
            else:
                act[n] = work.tile([P, nch, P], F32, name="a%d" % n, tag="act", bufs=3)
                dst = act[n][:]
            for c in range(nch):
                idx = 32 * j + cc + c
                nc.scalar.activation(out=dst[:, c, :], in_=mx[n][:, c, :], func=funcs[w],
                                     bias=bias_pp[:, idx:idx + 1], scale=1.0)

        def first(n):
            w, cc, nch, where, off, done, span = units[n]
            sl = slice(cc, cc + nch)
            if w == "r":
                pre[n] = work.tile([P, nch, P], F32, name="rh%d" % n, tag="pre", bufs=4)
                nc.vector.tensor_tensor(out=pre[n][:], in0=act[n][:], in1=h_t[:, sl, :], op=ALU.mult)
            elif w == "z":
                nc.vector.scalar_tensor_tensor(out=neg_a[:, sl, :], in0=z_t[:, sl, :], scalar=1.0, in1=h_t[:, sl, :],
                                               op0=ALU.subtract, op1=ALU.mult)
            else:
                t1 = work.tile([P, nch, P], F32, name="t1", tag="t1", bufs=2)
                nc.vector.scalar_tensor_tensor(out=t1[:], in0=act[n][:], scalar=alpha_pp[:, 0:1], in1=z_t[:, sl, :],
                                               op0=ALU.mult, op1=ALU.mult)
                pre[n] = work.tile([P, nch, P], F32, name="hn%d" % n, tag="pre", bufs=4)
                nc.vector.tensor_tensor(out=pre[n][:], in0=t1[:], in1=neg_a[:, sl, :], op=ALU.subtract)

        def flip_back(n):
            nch = units[n][2]
            back[n] = psum.tile([P, nch, P], F32, name="tb%d" % n, tag="tb")
            for c in range(nch):
                nc.tensor.transpose(back[n][:, c, :], pre[n][:, c, :], ident_f[:])

        def second(n):
            w, cc, nch, where, off, done, span = units[n]
            if w == "r":
                nc.vector.tensor_reduce(out=rhb[:, 32 * cc:32 * (cc + nch)],
                                        in_=back[n][:].rearrange("p c (n m) -> p (c n) m", m=M), axis=AX.X, op=ALU.add)
            else:
                nc.scalar.copy(out=hn_all[:, P * cc:P * (cc + nch)], in_=back[n][:].rearrange("p c j -> p (c j)"))
                if span is not None:
                    nc.sync.dma_start(out=out_1[:, span[0]:span[1]], in_=hn_all[:, span[0]:span[1]])

        def third(n):
            cc, nch = units[n][1], units[n][2]
            nc.vector.tensor_reduce(out=o0[:, 32 * cc:32 * (cc + nch)],
                                    in_=back[n][:].rearrange("p c (n m) -> p (c n) m", m=M), axis=AX.X, op=ALU.add)
            hi = P * (cc + nch)
            if hi == 3072:
                nc.sync.dma_start(out=out_0[:, 0:768], in_=o0[:, 0:768])
            elif hi == 4096:
                nc.sync.dma_start(out=out_0[:, 768:1024], in_=o0[:, 768:1024])

        total = len(units)
        flips = {3 + LAG + 1: 0, 7 + LAG + 1: 1}
        for n in range(total + LAG):
            if n < total:
                passes(n)
                for k in units[n][5]:
                    if k + RING < len(blocks):
                        load(k + RING)
            o = n - LAG
            turn = o >= 0 and units[o][0] != "z"
            if turn:
                flip_back(o)
            tp = None
            if n in flips:
                tp = flip_units(rhb, flips[n])
            if n < total:
                acts(n)
            if turn:
                second(o)
            if n in flips:
                grp = group_units(nc.scalar.copy, tp)
            if n < total:
                first(n)
            if n in flips:
                half = flips[n]
                quantise(grp, codes_r[:, P * half:P * (half + 1)], ascl_r[:, P * half:P * (half + 1)])
            if turn and units[o][0] == "h":
                third(o)
